import numpy as np
import ml_dtypes


def mxq(x, axis, fmt="e4m3"):
    dtype, down = {"e4m3": (ml_dtypes.float8_e4m3fn, 7), "e5m2": (ml_dtypes.float8_e5m2, 14)}[fmt]
    v = np.moveaxis(np.asarray(x, np.float32).astype(ml_dtypes.bfloat16).astype(np.float64), axis, -1)
    blocks = v.reshape(v.shape[:-1] + (-1, 32))
    amax = np.abs(blocks).max(-1, keepdims=True)
    byte = np.maximum(np.where(amax > 0, np.frexp(amax)[1] - 1 + 127, 0) - down, 1)
    scale = np.exp2(byte - 127.0)
    codes = (blocks / scale).astype(np.float32).astype(dtype).astype(np.float64)
    return np.moveaxis((codes * scale).reshape(v.shape), -1, axis)


WIDE = False


def mx_kscale(k):
    if not WIDE:
        return np.ones(k)
    levels = np.array([10, -10, 5, -5, 0])
    if k % 512:
        return np.exp2(np.random.permutation(np.resize(levels, k // 32))).repeat(32)
    a = np.empty((k // 512, 16))
    for p in range(k // 512):
        a[p, :8] = np.random.permutation(np.resize(levels, 8))
        for g in range(8):
            far = levels[np.abs(levels - a[p, g]) >= 10]
            a[p, g + 8] = far[np.random.randint(len(far))]
    return np.exp2(a.ravel()).repeat(32)


BF16 = ml_dtypes.bfloat16


def bf(x):
    return np.asarray(x, np.float32).astype(BF16)


def f64(x):
    return np.asarray(x).astype(np.float64)


B, S, E, H, HKV, W = 1, 1536, 1024, 8, 2, 512
D = E // H
THETA = 10000.0


def rope_tables():
    inv_freq = 1.0 / THETA ** (np.arange(0, D, 2) / D)
    ang = np.arange(S)[:, None] * inv_freq[None, :]
    ang = np.concatenate([ang, ang], axis=-1)
    return np.cos(ang), np.sin(ang)


def rotate_half(u):
    u1, u2 = np.split(u, 2, axis=-1)
    return np.concatenate([-u2, u1], axis=-1)


def heads(u, n):
    return u.reshape(B, S, n, D).transpose(0, 2, 1, 3)


def draw0():
    s = mx_kscale(E)
    c = 1.0 / np.sqrt(E)
    return {"hidden_states": bf(np.random.standard_normal((B, S, E)) * s),
            "q_w": bf(np.random.standard_normal((H * D, E)) * c / s),
            "k_w": bf(np.random.standard_normal((HKV * D, E)) * c / s),
            "v_w": bf(np.random.standard_normal((HKV * D, E)) * c / s)}


def core(hidden_states, q_w, k_w, v_w):
    xq = mxq(f64(hidden_states), 2, "e4m3")
    q = heads(xq @ mxq(f64(q_w), 1, "e4m3").T, H)
    k = heads(xq @ mxq(f64(k_w), 1, "e4m3").T, HKV)
    v = heads(xq @ mxq(f64(v_w), 1, "e4m3").T, HKV)
    cos, sin = rope_tables()
    return q * cos + rotate_half(q) * sin, k * cos + rotate_half(k) * sin, v


def e4m3fn_bytes(y):
    return np.clip(np.asarray(y, np.float64), -448.0, 448.0).astype(np.float32).astype(ml_dtypes.float8_e4m3fn).view(np.uint8)


def e4m3fn_values(b):
    return np.asarray(b, np.uint8).view(ml_dtypes.float8_e4m3fn).astype(np.float64)


def setup_inputs():
    d = draw0()
    x0 = np.asarray(d['hidden_states']).astype(np.float64)
    s = (np.max(np.abs(x0), axis=(0, 1), keepdims=True) / 448.0).astype(np.float32)
    out = {}
    for k, v in d.items():
        if k == 'hidden_states':
            out['hidden_states_bytes'] = e4m3fn_bytes(x0 / s.astype(np.float64))
            out['hidden_states_scale'] = s
        else:
            out[k] = v
    return out


def reference(hidden_states_bytes, hidden_states_scale, q_w, k_w, v_w):
    return core(e4m3fn_values(hidden_states_bytes) * hidden_states_scale.astype(np.float64), q_w, k_w, v_w)

@@ -1,0 +1,524 @@
+import math
+from contextlib import ExitStack
+
+import concourse.mybir as mybir
+from concourse.masks import make_identity
+
+F32 = mybir.dt.float32
+BF16 = mybir.dt.bfloat16
+U8 = mybir.dt.uint8
+U32 = mybir.dt.uint32
+I32 = mybir.dt.int32
+FP8 = mybir.dt.float8_e4m3fn
+FP8X4 = mybir.dt.float8_e4m3fn_x4
+ALU = mybir.AluOpType
+ACT = mybir.ActivationFunctionType
+
+S = 1536
+E = 1024
+P = 128
+NT = S // P
+NPAIR = NT // 2
+NPASS = E // 512
+HALF = 64
+THETA = 10000.0
+QF = 1024
+KF = 256
+RF = QF + KF
+OF = RF + KF
+QH = QF // P
+RH = RF // P
+
+FLOPS = 2 * S * E * OF
+SPAIR = 2
+FILL = 0
+TAIL = 5
+TAB = 0
+NW = 2
+W0N = 4
+WN = 2
+HEAD_BANKS = 16
+
+
+def tile_slidingwindowattention_pa_kernel(
+    tc, hidden_states_bytes, hidden_states_scale, q_w, k_w, v_w, out_0, out_1, out_2
+):
+    nc = tc.nc
+    with ExitStack() as ctx:
+        const = ctx.enter_context(tc.tile_pool(name="const", bufs=1))
+        xwp = ctx.enter_context(tc.tile_pool(name="xwp", bufs=4))
+        xgp = ctx.enter_context(tc.tile_pool(name="xgp", bufs=3))
+        outp = ctx.enter_context(tc.tile_pool(name="outp", bufs=3))
+        prodp = ctx.enter_context(tc.tile_pool(name="prodp", bufs=2))
+        psum = ctx.enter_context(tc.psum_pool(name="psum", bufs=8))
+
+        ctx.enter_context(tc.manual_schedule())
+
+        xsc = const.tile([P, NPASS, 1, 4], F32, name="xsc")
+        nc.sync.dma_start(
+            out=xsc[:, :, 0, :],
+            in_=hidden_states_scale.rearrange("a b (g p t) -> p (a b g) t", g=NPASS, p=P, t=4),
+        )
+        x_rows = hidden_states_bytes.rearrange("b (c p) k -> p (b c) k", p=P)
+        q_rows = q_w.rearrange("(a r) k -> r a k", r=P)
+        xsrc = {}
+        wsrc = {}
+
+        def load_x(lo, hi):
+            xb = const.tile([P, hi - lo, E], U8, name="xbytes%d" % lo)
+            nc.sync.dma_start(out=xb[:], in_=x_rows[:, lo:hi, :])
+            for c in range(lo, hi):
+                xsrc[c] = xb[:, c - lo, :]
+
+        def load_w(i):
+            wr = const.tile([P, 2, E], BF16, name="wraw%d" % i)
+            if i < 4:
+                nc.sync.dma_start(out=wr[:], in_=q_rows[:, 2 * i : 2 * i + 2, :])
+            elif i == 4:
+                nc.sync.dma_start(out=wr[:], in_=k_w.rearrange("(a r) k -> r a k", r=P))
+            else:
+                nc.sync.dma_start(out=wr[:], in_=v_w.rearrange("(a r) k -> r a k", r=P))
+            wsrc[2 * i] = wr[:, 0, :]
+            wsrc[2 * i + 1] = wr[:, 1, :]
+
+        load_x(0, 2)
+        load_x(2, 4)
+        for i in range(4):
+            load_w(i)
+        load_x(4, 6)
+        load_w(4)
+        load_w(5)
+        load_x(6, 8)
+        load_x(8, 12)
+
+        pos = const.tile([P, NT, 1], F32, name="pos")
+        nc.gpsimd.iota(
+            pos[:], pattern=[[P, NT]], base=0, channel_multiplier=1, allow_small_or_imprecise_dtypes=True
+        )
+        ident = const.tile([P, P], F32, name="ident")
+        make_identity(nc, ident[:])
+        warm = const.tile([P, 1], F32, name="warm")
+        nc.vector.memset(warm[:], 0.0)
+        warm2 = const.tile([P, 1], F32, name="warm2")
+        nc.scalar.activation(out=warm2[:], in_=warm[:], func=ACT.Sin)
+
+        wz = const.tile([P, 512], BF16, name="wz")
+        nc.gpsimd.memset(wz[:], 0.0)
+        nc.gpsimd.tensor_scalar(
+            out=wz[:, 0:8], in0=xsc[:].rearrange("p g o t -> p (g o t)"), scalar1=0.0, scalar2=0.0, op0=ALU.mult, op1=ALU.add
+        )
+
+        t_banks = [0]
+
+        def after_transposes():
+            t_banks[0] += 1
+            if t_banks[0] <= HEAD_BANKS and t_banks[0] % 2 == 0:
+                warm_pe(WN)
+
+        def warm_pe(n):
+            if n == 0:
+                return
+            t = psum.tile([P, 512], F32, name="pwarm", tag="bank")
+            for i in range(n):
+                nc.tensor.matmul(out=t[:], lhsT=wz[:, 0:P], rhs=wz[:], start=True, stop=True)
+
+        freq = const.tile([P, 1, HALF], F32, name="freq")
+        nc.vector.memset(freq[:, :, 0:1], 1.0)
+        for j in range(1, 8):
+            nc.vector.tensor_scalar(
+                out=freq[:, :, j : j + 1], in0=freq[:, :, 0:1], scalar1=THETA ** (-j / 64.0), scalar2=None, op0=ALU.mult
+            )
+        for m in (8, 16, 32):
+            nc.vector.tensor_scalar(
+                out=freq[:, :, m : 2 * m], in0=freq[:, :, 0:m], scalar1=THETA ** (-m / 64.0), scalar2=None, op0=ALU.mult
+            )
+        tshape = [P, NT, HALF]
+        ang = const.tile(tshape, F32, name="ang")
+        turns = const.tile(tshape, I32, name="turns")
+        red = const.tile(tshape, F32, name="red")
+        reda = const.tile(tshape, F32, name="reda")
+        sh = const.tile(tshape, F32, name="sh")
+        ch = const.tile(tshape, F32, name="ch")
+        prod = const.tile([P, NT, 1, HALF], F32, name="prod")
+        sq = const.tile([P, NT, 1, HALF], F32, name="sq")
+        rot_tab = const.tile([P, NT, 2, 1, P], F32, name="rot_tab")
+        tab_blocks = rot_tab[:].rearrange("p c r o (w d) -> p c (r o w) d", d=HALF)
+
+        def table_v(a, b):
+            shp = [P, b - a, HALF]
+            nc.vector.tensor_tensor(
+                out=ang[:, a:b], in0=pos[:, a:b].to_broadcast(shp), in1=freq[:].to_broadcast(shp), op=ALU.mult
+            )
+            nc.vector.tensor_scalar(
+                out=turns[:, a:b], in0=ang[:, a:b], scalar1=1.0 / (2.0 * math.pi), scalar2=0.25, op0=ALU.mult, op1=ALU.add
+            )
+            nc.vector.scalar_tensor_tensor(
+                out=red[:, a:b], in0=turns[:, a:b], scalar=-2.0 * math.pi, in1=ang[:, a:b], op0=ALU.mult, op1=ALU.add
+            )
+            nc.vector.scalar_tensor_tensor(
+                out=reda[:, a:b], in0=red[:, a:b], scalar=-1.0, in1=red[:, a:b], op0=ALU.mult, op1=ALU.max
+            )
+
+        def table_t(a, b):
+            nc.scalar.activation(out=turns[:, a:b].bitcast(U32), in_=ang[:, a:b], func=ACT.Copy, bias=0.25, scale=1.0 / (2.0 * math.pi))
+
+        def table_a(a, b):
+            shp = [P, b - a, HALF]
+            nc.vector.tensor_tensor(
+                out=ang[:, a:b], in0=pos[:, a:b].to_broadcast(shp), in1=freq[:].to_broadcast(shp), op=ALU.mult
+            )
+
+        def table_r(a, b):
+            nc.vector.scalar_tensor_tensor(
+                out=red[:, a:b], in0=turns[:, a:b], scalar=-2.0 * math.pi, in1=ang[:, a:b], op0=ALU.mult, op1=ALU.add
+            )
+
+        def table_s2(a, b):
+            nc.scalar.activation(out=sh[:, a:b], in_=red[:, a:b], func=ACT.Sin, scale=0.5)
+            nc.scalar.activation(out=reda[:, a:b], in_=red[:, a:b], func=ACT.Abs)
+            nc.scalar.activation(out=ch[:, a:b], in_=reda[:, a:b], func=ACT.Sin, bias=math.pi / 2.0, scale=-0.5)
+
+        def table_s(a, b):
+            nc.scalar.activation(out=sh[:, a:b], in_=red[:, a:b], func=ACT.Sin, scale=0.5)
+            nc.scalar.activation(out=ch[:, a:b], in_=reda[:, a:b], func=ACT.Sin, bias=math.pi / 2.0, scale=-0.5)
+
+        def table_p(a, b):
+            n = b - a
+            nc.vector.scalar_tensor_tensor(
+                out=sq[:, a:b, 0, :], in0=sh[:, a:b], scalar=-2.0, in1=sh[:, a:b], op0=ALU.mult, op1=ALU.mult
+            )
+            nc.vector.scalar_tensor_tensor(
+                out=tab_blocks[:, a:b, 1, :], in0=sh[:, a:b], scalar=-2.0, in1=ch[:, a:b], op0=ALU.mult, op1=ALU.mult
+            )
+            nc.vector.scalar_tensor_tensor(
+                out=tab_blocks[:, a:b, 2, :], in0=sh[:, a:b], scalar=2.0, in1=ch[:, a:b], op0=ALU.mult, op1=ALU.mult
+            )
+            nc.vector.tensor_scalar(
+                out=tab_blocks[:, a:b, 0:4:3, :],
+                in0=sq[:, a:b].to_broadcast([P, n, 2, HALF]),
+                scalar1=1.0,
+                scalar2=None,
+                op0=ALU.add,
+            )
+
+        def table_g(a, b):
+            nc.gpsimd.tensor_tensor(out=sq[:, a:b, 0, :], in0=sh[:, a:b], in1=sh[:, a:b], op=ALU.mult)
+            nc.gpsimd.tensor_tensor(out=prod[:, a:b, 0, :], in0=sh[:, a:b], in1=ch[:, a:b], op=ALU.mult)
+            nc.gpsimd.tensor_scalar(
+                out=tab_blocks[:, a:b, 0:4:3, :],
+                in0=sq[:, a:b].to_broadcast([P, b - a, 2, HALF]),
+                scalar1=-2.0,
+                scalar2=1.0,
+                op0=ALU.mult,
+                op1=ALU.add,
+            )
+            nc.gpsimd.tensor_scalar(
+                out=tab_blocks[:, a:b, 1, :], in0=prod[:, a:b, 0, :], scalar1=-2.0, scalar2=0.0, op0=ALU.mult, op1=ALU.add
+            )
+            nc.gpsimd.tensor_scalar(
+                out=tab_blocks[:, a:b, 2, :], in0=prod[:, a:b, 0, :], scalar1=2.0, scalar2=0.0, op0=ALU.mult, op1=ALU.add
+            )
+
+        xw = {}
+        xtp = {}
+        xg = {}
+        xq = {}
+        xs8 = {}
+        wtp = {}
+        wg = {}
+        wq = {}
+        ws8 = {}
+
+        def x_cast(c):
+            t = xwp.tile([P, E], BF16, name="xw", tag="xw")
+            nc.scalar.copy(out=t[:], in_=xsrc[c].bitcast(FP8))
+            xw[c] = t
+
+        def x_transpose(pair, g):
+            tp = psum.tile([P, 2, 2, P], F32, name="xtp", tag="bank")
+            for cc in range(2):
+                words = xw[2 * pair + cc][:].bitcast(F32)
+                for u in range(2):
+                    nc.tensor.transpose(tp[:, u, cc, :], words[:, 256 * g + u : 256 * (g + 1) : 2], ident[:])
+            xtp[(pair, g)] = tp
+            after_transposes()
+
+        def x_scale_s(pair, g):
+            src = xtp[(pair, g)][:].rearrange("p u c n -> p u (c n)").bitcast(BF16).rearrange("p u (n e) -> p u e n", e=2)
+            for u in range(2):
+                for e in range(2):
+                    t = 2 * u + e
+                    nc.scalar.activation(
+                        out=xg[pair][:, g, :, t], in_=src[:, u, e, :], func=ACT.Copy, scale=xsc[:, g, 0, t : t + 1]
+                    )
+
+        def x_scale(pair, g):
+            if pair not in xg:
+                xg[pair] = xgp.tile([P, NPASS, 2 * P, 4], BF16, name="xg", tag="xg", align_bytes=64)
+            if g == 1 and pair >= SPAIR:
+                x_scale_s(pair, g)
+                return
+            nc.vector.tensor_tensor(
+                out=xg[pair][:, g].rearrange("p n (u e) -> p n u e", e=2),
+                in0=xtp[(pair, g)][:].rearrange("p u c n -> p u (c n)").bitcast(BF16).rearrange("p u (n e) -> p n u e", e=2),
+                in1=xsc[:, g].rearrange("p o (u e) -> p o u e", e=2).to_broadcast([P, 2 * P, 2, 2]),
+                op=ALU.mult,
+            )
+
+        def x_quant(pair):
+            q = const.tile([P, NPASS * 2 * P], U32, name="xq%d" % pair, align_bytes=64)
+            s = const.tile([P, NPASS * 2 * P], U8, name="xs%d" % pair, align_bytes=64)
+            nc.vector.quantize_mx(
+                out=q[:].bitcast(FP8X4), scales=s[:], in_=xg[pair][:].rearrange("p g n t -> p (g n t)")
+            )
+            xq[pair] = q
+            xs8[pair] = s
+
+        def w_transpose(a):
+            words = wsrc[a].bitcast(F32)
+            tp = psum.tile([P, NPASS, 2, P], F32, name="wtp", tag="bank")
+            for g in range(NPASS):
+                for u in range(2):
+                    nc.tensor.transpose(tp[:, g, u, :], words[:, 256 * g + u : 256 * (g + 1) : 2], ident[:])
+            wtp[a] = tp
+            after_transposes()
+
+        def w_evac(a):
+            j = a // 4
+            if a % 4 == 0:
+                wg[j] = const.tile([P, NPASS, 512, 4], BF16, name="wg%d" % j, align_bytes=64)
+            wg_words = (
+                wg[j][:].rearrange("p g f t -> p (g f t)").bitcast(F32).rearrange("p (g f u) -> p g f u", g=NPASS, u=2)
+            )
+            r0 = P * (a % 4)
+            nc.scalar.copy(out=wg_words[:, :, r0 : r0 + P, :], in_=wtp[a][:].rearrange("p g u r -> p g r u"))
+
+        def w_quant(j, g):
+            if g == 1:
+                return
+            wq[j] = const.tile([P, NPASS, 512], U32, name="wq%d" % j, align_bytes=64)
+            ws8[j] = const.tile([P, NPASS, 512], U8, name="ws%d" % j, align_bytes=64)
+            nc.vector.quantize_mx(
+                out=wq[j][:].rearrange("p g f -> p (g f)").bitcast(FP8X4),
+                scales=ws8[j][:].rearrange("p g f -> p (g f)"),
+                in_=wg[j][:].rearrange("p g f t -> p (g f t)"),
+            )
+
+        def mm(out, pair, cc, j, lo, hi):
+            for g in range(NPASS):
+                xcols = slice(P * (2 * g + cc), P * (2 * g + cc + 1))
+                nc.tensor.matmul_mx(
+                    out=out,
+                    lhsT=xq[pair][:, xcols].bitcast(FP8X4),
+                    lhsT_scale=xs8[pair][:, xcols],
+                    rhs=wq[j][:, g, lo:hi].bitcast(FP8X4),
+                    rhs_scale=ws8[j][:, g, lo:hi],
+                    start=(g == 0),
+                    stop=(g == NPASS - 1),
+                )
+
+        q_out = out_0.rearrange("b h (c p) d -> c p (b h) d", p=P)
+        k_out = out_1.rearrange("b h (c p) d -> c p (b h) d", p=P)
+        v_out = out_2.rearrange("b h (c p) d -> c p (b h) d", p=P)
+        res = {}
+        prods = {}
+        acc = {}
+
+        def begin(pair):
+            res[pair] = outp.tile([P, 2, OF], F32, name="res", tag="res")
+            prods[pair] = prodp.tile([P, 2, 2, RF], F32, name="prods", tag="prods")
+
+        def mm_q(pair, cc, j):
+            ps = psum.tile([P, 1, 4, P], F32, name="ps", tag="bank")
+            mm(ps[:].rearrange("p o h x -> p (o h x)"), pair, cc, j, 0, 512)
+            acc[(pair, cc, j)] = ps
+
+        def rope_q(pair, cc, j):
+            nc.vector.tensor_tensor(
+                out=prods[pair][:, cc, :, 512 * j : 512 * (j + 1)].rearrange("p r (h x) -> p r h x", x=P),
+                in0=acc[(pair, cc, j)][:].to_broadcast([P, 2, 4, P]),
+                in1=rot_tab[:, 2 * pair + cc].to_broadcast([P, 2, 4, P]),
+                op=ALU.mult,
+            )
+
+        def mm_k(pair):
+            psk = psum.tile([P, 2, 2, P], F32, name="psk", tag="bank")
+            for cc in range(2):
+                mm(psk[:, cc].rearrange("p h x -> p (h x)"), pair, cc, 2, 0, KF)
+            acc[(pair, "k")] = psk
+
+        def rope_k(pair):
+            for r in range(2):
+                nc.vector.tensor_tensor(
+                    out=prods[pair][:, :, r, QF:RF].rearrange("p c (h x) -> p c h x", x=P),
+                    in0=acc[(pair, "k")][:],
+                    in1=rot_tab[:, 2 * pair : 2 * pair + 2, r].to_broadcast([P, 2, 2, P]),
+                    op=ALU.mult,
+                )
+
+        def mm_v(pair):
+            psv = psum.tile([P, 2, KF], F32, name="psv", tag="bank")
+            for cc in range(2):
+                mm(psv[:, cc, :], pair, cc, 2, KF, 2 * KF)
+            acc[(pair, "v")] = psv
+
+        def copy_v(pair):
+            nc.scalar.copy(out=res[pair][:, :, RF:OF], in_=acc[(pair, "v")][:])
+            for cc in range(2):
+                nc.sync.dma_start(
+                    out=v_out[2 * pair + cc], in_=res[pair][:, cc, RF:OF].rearrange("p (h d) -> p h d", d=P)
+                )
+
+        def add(pair, cc, h0, h1, eng=None):
+            u = prods[pair][:, cc, :, P * h0 : P * h1].rearrange("p r (h w d) -> p r h w d", w=2, d=HALF)
+            (eng or nc.gpsimd).tensor_tensor(
+                out=res[pair][:, cc, P * h0 : P * h1].rearrange("p (h r d) -> p r h d", r=2, d=HALF),
+                in0=u[:, :, :, 0, :],
+                in1=u[:, :, :, 1, :],
+                op=ALU.add,
+            )
+            c = 2 * pair + cc
+            if h0 < QH:
+                hq = min(h1, QH)
+                nc.sync.dma_start(
+                    out=q_out[c][:, h0:hq, :], in_=res[pair][:, cc, P * h0 : P * hq].rearrange("p (h d) -> p h d", d=P)
+                )
+            if h1 > QH:
+                nc.sync.dma_start(out=k_out[c], in_=res[pair][:, cc, QF:RF].rearrange("p (h d) -> p h d", d=P))
+
+        if TAB == 0:
+            table_v(0, 6)
+            table_s(0, 6)
+            table_v(6, 12)
+            table_p(0, 6)
+        else:
+            table_v(0, 2)
+            table_s(0, 2)
+            table_g(0, 2)
+            table_v(2, 6)
+            table_s(2, 6)
+            table_g(2, 6)
+            table_v(6, 12)
+        for c in range(4):
+            x_cast(c)
+        warm_pe(W0N)
+        x_transpose(0, 0)
+        x_transpose(0, 1)
+        w_transpose(0)
+        x_transpose(1, 0)
+        x_transpose(1, 1)
+        for a in range(1, 4):
+            w_transpose(a)
+        for a in range(4):
+            w_evac(a)
+        x_scale(0, 0)
+        x_scale(0, 1)
+        x_scale(1, 0)
+        x_quant(0)
+        x_scale(1, 1)
+        w_quant(0, 0)
+        x_quant(1)
+        begin(0)
+        begin(1)
+        for a in range(4, 4 + NW):
+            w_transpose(a)
+        mm_q(0, 0, 0)
+        mm_q(0, 1, 0)
+        for a in range(4 + NW, 8):
+            w_transpose(a)
+        for a in range(4, 8):
+            w_evac(a)
+        table_s(6, 12)
+        if TAB == 1:
+            table_g(6, 12)
+        rope_q(0, 0, 0)
+        rope_q(0, 1, 0)
+        w_quant(1, 0)
+        for a in range(8, 12):
+            w_transpose(a)
+        mm_q(0, 0, 1)
+        mm_q(0, 1, 1)
+        for a in range(8, 12):
+            w_evac(a)
+        x_cast(4)
+        x_cast(5)
+        if TAB == 0:
+            table_p(6, 12)
+        w_quant(2, 0)
+        rope_q(0, 0, 1)
+        add(0, 0, 0, QH)
+        rope_q(0, 1, 1)
+        add(0, 1, 0, QH)
+
+        for pair in range(NPAIR):
+            last = pair == NPAIR - 1
+            nxt = pair + 1
+            prep = 2 <= nxt < NPAIR
+            if pair > 1:
+                begin(pair)
+            if prep:
+                x_transpose(nxt, 1)
+                x_transpose(nxt, 0)
+                if SPAIR <= nxt:
+                    x_scale(nxt, 1)
+            if 3 <= pair + 2 < NPAIR:
+                x_cast(2 * pair + 4)
+                x_cast(2 * pair + 5)
+            mm_k(pair)
+            mm_v(pair)
+            if pair > 1 or (pair == 1 and not FILL):
+                mm_q(pair, 0, 0)
+            if pair > 0:
+                mm_q(pair, 0, 1)
+                mm_q(pair, 1, 0)
+                mm_q(pair, 1, 1)
+            if prep:
+                x_scale(nxt, 0)
+            rope_k(pair)
+            copy_v(pair)
+            if pair == 0:
+                add(pair, 0, QH, RH)
+                add(pair, 1, QH, RH)
+            if prep and SPAIR > nxt:
+                x_scale(nxt, 1)
+            if pair > 1 or (pair == 1 and not FILL):
+                rope_q(pair, 0, 0)
+            if prep:
+                x_quant(nxt)
+            if pair > 0:
+                rope_q(pair, 0, 1)
+                if not last:
+                    add(pair, 0, 0, RH)
+                    rope_q(pair, 1, 0)
+                    rope_q(pair, 1, 1)
+                    add(pair, 1, 0, RH)
+                elif TAIL == 0:
+                    add(pair, 0, 0, RH)
+                    rope_q(pair, 1, 0)
+                    add(pair, 1, QH, RH)
+                    add(pair, 1, 0, 4)
+                    rope_q(pair, 1, 1)
+                    add(pair, 1, 4, QH)
+                elif TAIL == 3:
+                    add(pair, 0, 0, RH)
+                    rope_q(pair, 1, 0)
+                    rope_q(pair, 1, 1)
+                    add(pair, 1, 0, RH, nc.vector)
+                elif TAIL == 4:
+                    add(pair, 0, 0, RH, nc.vector)
+                    rope_q(pair, 1, 0)
+                    rope_q(pair, 1, 1)
+                    add(pair, 1, 0, RH, nc.vector)
+                elif TAIL == 5:
+                    add(pair, 0, 0, RH, nc.vector)
+                    rope_q(pair, 1, 0)
+                    add(pair, 1, QH, RH)
+                    add(pair, 1, 0, 4)
+                    rope_q(pair, 1, 1)
+                    add(pair, 1, 4, QH, nc.vector)
+                elif TAIL == 6:
+                    add(pair, 0, 0, RH)
+                    rope_q(pair, 1, 0)
+                    rope_q(pair, 1, 1)
+                    add(pair, 1, 4, RH, nc.vector)
+                    add(pair, 1, 0, 4, nc.vector)

@@ -485,13 +485,16 @@ def tile_slidingwindowattention_pa_kernel(
                 rope_q(pair, 0, 0)
             if prep:
                 x_quant(nxt)
+            if pair > 0 and not last:
+                add(pair, 0, 0, 4)
             if pair > 0:
                 rope_q(pair, 0, 1)
                 if not last:
-                    add(pair, 0, 0, RH)
+                    add(pair, 0, 4, RH)
                     rope_q(pair, 1, 0)
+                    add(pair, 1, 0, 4)
                     rope_q(pair, 1, 1)
-                    add(pair, 1, 0, RH)
+                    add(pair, 1, 4, RH)
                 elif TAIL == 0:
                     add(pair, 0, 0, RH)
                     rope_q(pair, 1, 0)

@@ -104,9 +104,6 @@ def tile_slidingwindowattention_pa_kernel(
 
         wz = const.tile([P, 512], BF16, name="wz")
         nc.gpsimd.memset(wz[:], 0.0)
-        nc.gpsimd.tensor_scalar(
-            out=wz[:, 0:8], in0=xsc[:].rearrange("p g o t -> p (g o t)"), scalar1=0.0, scalar2=0.0, op0=ALU.mult, op1=ALU.add
-        )
 
         t_banks = [0]
 
@@ -389,6 +386,7 @@ def tile_slidingwindowattention_pa_kernel(
         if TAB == 0:
             table_v(0, 6)
             table_s(0, 6)
+            nc.scalar.copy(out=wz[:, 0:8], in_=sh[:, 0, 0:8])
             table_v(6, 12)
             table_p(0, 6)
         else:

@@ -156,6 +156,27 @@ def tile_slidingwindowattention_pa_kernel(
                 out=reda[:, a:b], in0=red[:, a:b], scalar=-1.0, in1=red[:, a:b], op0=ALU.mult, op1=ALU.max
             )
 
+        def tv_ang(a, b):
+            shp = [P, b - a, HALF]
+            nc.vector.tensor_tensor(
+                out=ang[:, a:b], in0=pos[:, a:b].to_broadcast(shp), in1=freq[:].to_broadcast(shp), op=ALU.mult
+            )
+
+        def tv_turns(a, b):
+            nc.vector.tensor_scalar(
+                out=turns[:, a:b], in0=ang[:, a:b], scalar1=1.0 / (2.0 * math.pi), scalar2=0.25, op0=ALU.mult, op1=ALU.add
+            )
+
+        def tv_red(a, b):
+            nc.vector.scalar_tensor_tensor(
+                out=red[:, a:b], in0=turns[:, a:b], scalar=-2.0 * math.pi, in1=ang[:, a:b], op0=ALU.mult, op1=ALU.add
+            )
+
+        def tv_abs(a, b):
+            nc.vector.scalar_tensor_tensor(
+                out=reda[:, a:b], in0=red[:, a:b], scalar=-1.0, in1=red[:, a:b], op0=ALU.mult, op1=ALU.max
+            )
+
         def table_t(a, b):
             nc.scalar.activation(out=turns[:, a:b].bitcast(U32), in_=ang[:, a:b], func=ACT.Copy, bias=0.25, scale=1.0 / (2.0 * math.pi))
 
@@ -384,10 +405,11 @@ def tile_slidingwindowattention_pa_kernel(
                 nc.sync.dma_start(out=k_out[c], in_=res[pair][:, cc, QF:RF].rearrange("p (h d) -> p h d", d=P))
 
         if TAB == 0:
-            table_v(0, 6)
+            for step in (tv_ang, tv_turns, tv_red, tv_abs):
+                step(0, 6)
+                step(6, 12)
             table_s(0, 6)
             nc.scalar.copy(out=wz[:, 0:8], in_=sh[:, 0, 0:8])
-            table_v(6, 12)
             table_p(0, 6)
         else:
             table_v(0, 2)

@@ -98,9 +98,7 @@ def tile_slidingwindowattention_pa_kernel(
         ident = const.tile([P, P], F32, name="ident")
         make_identity(nc, ident[:])
         warm = const.tile([P, 1], F32, name="warm")
-        nc.vector.memset(warm[:], 0.0)
         warm2 = const.tile([P, 1], F32, name="warm2")
-        nc.scalar.activation(out=warm2[:], in_=warm[:], func=ACT.Sin)
 
         wz = const.tile([P, 512], BF16, name="wz")
         nc.gpsimd.memset(wz[:], 0.0)
@@ -120,15 +118,20 @@ def tile_slidingwindowattention_pa_kernel(
                 nc.tensor.matmul(out=t[:], lhsT=wz[:, 0:P], rhs=wz[:], start=True, stop=True)
 
         freq = const.tile([P, 1, HALF], F32, name="freq")
-        nc.vector.memset(freq[:, :, 0:1], 1.0)
-        for j in range(1, 8):
-            nc.vector.tensor_scalar(
-                out=freq[:, :, j : j + 1], in0=freq[:, :, 0:1], scalar1=THETA ** (-j / 64.0), scalar2=None, op0=ALU.mult
-            )
-        for m in (8, 16, 32):
-            nc.vector.tensor_scalar(
-                out=freq[:, :, m : 2 * m], in0=freq[:, :, 0:m], scalar1=THETA ** (-m / 64.0), scalar2=None, op0=ALU.mult
-            )
+        fab = const.tile([P, 2, 1, 1, 8], F32, name="fab")
+        nc.vector.memset(fab[:], 1.0)
+        nc.vector.memset(warm[:], 0.0)
+        nc.scalar.activation(out=warm2[:], in_=warm[:], func=ACT.Sin)
+        for row in (1, 0):
+            for j in range(1, 8):
+                nc.vector.tensor_scalar(
+                    out=fab[:, row, 0, :, j : j + 1],
+                    in0=fab[:, 0, 0, :, 0:1],
+                    scalar1=THETA ** (-j * (8 if row else 1) / 64.0),
+                    scalar2=None,
+                    op0=ALU.mult,
+                )
+        posb = const.tile([P, NT, 8, 1], F32, name="posb")
         tshape = [P, NT, HALF]
         ang = const.tile(tshape, F32, name="ang")
         turns = const.tile(tshape, I32, name="turns")
@@ -156,10 +159,22 @@ def tile_slidingwindowattention_pa_kernel(
                 out=reda[:, a:b], in0=red[:, a:b], scalar=-1.0, in1=red[:, a:b], op0=ALU.mult, op1=ALU.max
             )
 
-        def tv_ang(a, b):
-            shp = [P, b - a, HALF]
+        def tv_posb(a, b):
+            shp = [P, b - a, 8, 1]
             nc.vector.tensor_tensor(
-                out=ang[:, a:b], in0=pos[:, a:b].to_broadcast(shp), in1=freq[:].to_broadcast(shp), op=ALU.mult
+                out=posb[:, a:b],
+                in0=pos[:, a:b].rearrange("p c (o i) -> p c o i", i=1).to_broadcast(shp),
+                in1=fab[:, 1].rearrange("p a b j -> p a j b").to_broadcast(shp),
+                op=ALU.mult,
+            )
+
+        def tv_ang(a, b):
+            shp = [P, b - a, 8, 8]
+            nc.vector.tensor_tensor(
+                out=ang[:, a:b].rearrange("p c (i j) -> p c i j", j=8),
+                in0=posb[:, a:b].to_broadcast(shp),
+                in1=fab[:, 0].to_broadcast(shp),
+                op=ALU.mult,
             )
 
         def tv_turns(a, b):
@@ -259,6 +274,17 @@ def tile_slidingwindowattention_pa_kernel(
                 for u in range(2):
                     nc.tensor.transpose(tp[:, u, cc, :], words[:, 256 * g + u : 256 * (g + 1) : 2], ident[:])
             xtp[(pair, g)] = tp
+            after_transposes()
+
+        def x_transpose_first():
+            for g in range(NPASS):
+                xtp[(0, g)] = psum.tile([P, 2, 2, P], F32, name="xtp", tag="bank")
+            for cc in range(2):
+                words = xw[cc][:].bitcast(F32)
+                for g in range(NPASS):
+                    for u in range(2):
+                        nc.tensor.transpose(xtp[(0, g)][:, u, cc, :], words[:, 256 * g + u : 256 * (g + 1) : 2], ident[:])
+            after_transposes()
             after_transposes()
 
         def x_scale_s(pair, g):
@@ -405,9 +431,10 @@ def tile_slidingwindowattention_pa_kernel(
                 nc.sync.dma_start(out=k_out[c], in_=res[pair][:, cc, QF:RF].rearrange("p (h d) -> p h d", d=P))
 
         if TAB == 0:
-            for step in (tv_ang, tv_turns, tv_red, tv_abs):
+            for step in (tv_posb, tv_ang, tv_turns, tv_red, tv_abs):
                 step(0, 6)
                 step(6, 12)
+            x_cast(0)
             table_s(0, 6)
             nc.scalar.copy(out=wz[:, 0:8], in_=sh[:, 0, 0:8])
             table_p(0, 6)
@@ -419,11 +446,10 @@ def tile_slidingwindowattention_pa_kernel(
             table_s(2, 6)
             table_g(2, 6)
             table_v(6, 12)
-        for c in range(4):
+        for c in range(1, 4):
             x_cast(c)
         warm_pe(W0N)
-        x_transpose(0, 0)
-        x_transpose(0, 1)
+        x_transpose_first()
         w_transpose(0)
         x_transpose(1, 0)
         x_transpose(1, 1)

@@ -179,7 +179,7 @@ def tile_slidingwindowattention_pa_kernel(
 
         def tv_turns(a, b):
             nc.vector.tensor_scalar(
-                out=turns[:, a:b], in0=ang[:, a:b], scalar1=1.0 / (2.0 * math.pi), scalar2=0.25, op0=ALU.mult, op1=ALU.add
+                out=turns[:, a:b], in0=ang[:, a:b], scalar1=1.0 / (2.0 * math.pi), scalar2=-0.125, op0=ALU.mult, op1=ALU.add
             )
 
         def tv_red(a, b):
@@ -213,7 +213,7 @@ def tile_slidingwindowattention_pa_kernel(
 
         def table_s(a, b):
             nc.scalar.activation(out=sh[:, a:b], in_=red[:, a:b], func=ACT.Sin, scale=0.5)
-            nc.scalar.activation(out=ch[:, a:b], in_=reda[:, a:b], func=ACT.Sin, bias=math.pi / 2.0, scale=-0.5)
+            nc.scalar.activation(out=ch[:, a:b], in_=red[:, a:b], func=ACT.Sin, bias=math.pi / 2.0, scale=-0.5)
 
         def table_p(a, b):
             n = b - a
@@ -223,15 +223,15 @@ def tile_slidingwindowattention_pa_kernel(
             nc.vector.scalar_tensor_tensor(
                 out=tab_blocks[:, a:b, 1, :], in0=sh[:, a:b], scalar=-2.0, in1=ch[:, a:b], op0=ALU.mult, op1=ALU.mult
             )
-            nc.vector.scalar_tensor_tensor(
-                out=tab_blocks[:, a:b, 2, :], in0=sh[:, a:b], scalar=2.0, in1=ch[:, a:b], op0=ALU.mult, op1=ALU.mult
-            )
             nc.vector.tensor_scalar(
                 out=tab_blocks[:, a:b, 0:4:3, :],
                 in0=sq[:, a:b].to_broadcast([P, n, 2, HALF]),
                 scalar1=1.0,
                 scalar2=None,
                 op0=ALU.add,
+            )
+            nc.vector.tensor_scalar(
+                out=tab_blocks[:, a:b, 2, :], in0=tab_blocks[:, a:b, 1, :], scalar1=-1.0, scalar2=None, op0=ALU.mult
             )
 
         def table_g(a, b):
@@ -265,6 +265,11 @@ def tile_slidingwindowattention_pa_kernel(
         def x_cast(c):
             t = xwp.tile([P, E], BF16, name="xw", tag="xw")
             nc.scalar.copy(out=t[:], in_=xsrc[c].bitcast(FP8))
+            xw[c] = t
+
+        def x_cast_v(c):
+            t = xwp.tile([P, E], BF16, name="xw", tag="xw")
+            nc.vector.tensor_copy(out=t[:], in_=xsrc[c].bitcast(FP8))
             xw[c] = t
 
         def x_transpose(pair, g):
@@ -431,13 +436,15 @@ def tile_slidingwindowattention_pa_kernel(
                 nc.sync.dma_start(out=k_out[c], in_=res[pair][:, cc, QF:RF].rearrange("p (h d) -> p h d", d=P))
 
         if TAB == 0:
-            for step in (tv_posb, tv_ang, tv_turns, tv_red, tv_abs):
+            nc.scalar.copy(out=wz[:, 0:8], in_=xsc[:].rearrange("p g o t -> p (g o t)"))
+            x_cast(0)
+            for step in (tv_posb, tv_ang, tv_turns):
                 step(0, 6)
                 step(6, 12)
-            x_cast(0)
+            x_cast_v(1)
+            tv_red(0, 6)
+            tv_red(6, 12)
             table_s(0, 6)
-            nc.scalar.copy(out=wz[:, 0:8], in_=sh[:, 0, 0:8])
-            table_p(0, 6)
         else:
             table_v(0, 2)
             table_s(0, 2)
@@ -446,10 +453,11 @@ def tile_slidingwindowattention_pa_kernel(
             table_s(2, 6)
             table_g(2, 6)
             table_v(6, 12)
-        for c in range(1, 4):
+        for c in range(2, 4):
             x_cast(c)
         warm_pe(W0N)
-        x_transpose_first()
+        x_transpose(0, 0)
+        x_transpose(0, 1)
         w_transpose(0)
         x_transpose(1, 0)
         x_transpose(1, 1)
@@ -459,6 +467,7 @@ def tile_slidingwindowattention_pa_kernel(
             w_evac(a)
         x_scale(0, 0)
         x_scale(0, 1)
+        table_p(0, 6)
         x_scale(1, 0)
         x_quant(0)
         x_scale(1, 1)

@@ -31,8 +31,10 @@ RH = RF // P
 
 FLOPS = 2 * S * E * OF
 SPAIR = 2
+SPAIR0 = 9
+QLATE = 0
 FILL = 0
-TAIL = 5
+TAIL = 18
 TAB = 0
 NW = 2
 W0N = 4
@@ -304,7 +306,7 @@ def tile_slidingwindowattention_pa_kernel(
         def x_scale(pair, g):
             if pair not in xg:
                 xg[pair] = xgp.tile([P, NPASS, 2 * P, 4], BF16, name="xg", tag="xg", align_bytes=64)
-            if g == 1 and pair >= SPAIR:
+            if (g == 1 and pair >= SPAIR) or (g == 0 and pair >= SPAIR0):
                 x_scale_s(pair, g)
                 return
             nc.vector.tensor_tensor(
@@ -418,6 +420,22 @@ def tile_slidingwindowattention_pa_kernel(
                     out=v_out[2 * pair + cc], in_=res[pair][:, cc, RF:OF].rearrange("p (h d) -> p h d", d=P)
                 )
 
+        def pe_add(pair, cc, h0, h1):
+            pad = psum.tile([P, P * (h1 - h0)], F32, name="pad", tag="bank")
+            u = prods[pair][:, cc, :, P * h0 : P * h1].rearrange("p r (h w d) -> p w h r d", w=2, d=HALF)
+            for w in range(2):
+                nc.tensor.matmul(
+                    out=pad[:].rearrange("p (h r d) -> p h r d", r=2, d=HALF),
+                    lhsT=ident[:],
+                    rhs=u[:, w],
+                    start=(w == 0),
+                    stop=(w == 1),
+                )
+            nc.scalar.copy(out=res[pair][:, cc, P * h0 : P * h1], in_=pad[:])
+            nc.sync.dma_start(
+                out=q_out[2 * pair + cc][:, h0:h1, :], in_=res[pair][:, cc, P * h0 : P * h1].rearrange("p (h d) -> p h d", d=P)
+            )
+
         def add(pair, cc, h0, h1, eng=None):
             u = prods[pair][:, cc, :, P * h0 : P * h1].rearrange("p r (h w d) -> p r h w d", w=2, d=HALF)
             (eng or nc.gpsimd).tensor_tensor(
@@ -501,9 +519,11 @@ def tile_slidingwindowattention_pa_kernel(
             table_p(6, 12)
         w_quant(2, 0)
         rope_q(0, 0, 1)
-        add(0, 0, 0, QH)
+        add(0, 0, 0, 4)
+        add(0, 0, 4, QH)
         rope_q(0, 1, 1)
-        add(0, 1, 0, QH)
+        add(0, 1, 0, 4)
+        add(0, 1, 4, QH)
 
         for pair in range(NPAIR):
             last = pair == NPAIR - 1
@@ -538,15 +558,20 @@ def tile_slidingwindowattention_pa_kernel(
                 x_scale(nxt, 1)
             if pair > 1 or (pair == 1 and not FILL):
                 rope_q(pair, 0, 0)
-            if prep:
+            if prep and nxt < SPAIR0:
                 x_quant(nxt)
-            if pair > 0 and not last:
+            if last and TAIL == 11:
+                add(pair, 0, QH, RH)
+                add(pair, 1, QH, RH)
+            if pair > 0 and (not last or 10 <= TAIL <= 15):
                 add(pair, 0, 0, 4)
             if pair > 0:
                 rope_q(pair, 0, 1)
                 if not last:
                     add(pair, 0, 4, RH)
                     rope_q(pair, 1, 0)
+                    if prep and nxt >= SPAIR0:
+                        x_quant(nxt)
                     add(pair, 1, 0, 4)
                     rope_q(pair, 1, 1)
                     add(pair, 1, 4, RH)
@@ -573,6 +598,53 @@ def tile_slidingwindowattention_pa_kernel(
                     add(pair, 1, QH, RH)
                     add(pair, 1, 0, 4)
                     rope_q(pair, 1, 1)
+                    add(pair, 1, 4, QH, nc.vector)
+                elif TAIL == 10:
+                    pe_add(pair, 0, 4, QH)
+                    add(pair, 0, QH, RH)
+                    rope_q(pair, 1, 0)
+                    add(pair, 1, QH, RH)
+                    add(pair, 1, 0, 4)
+                    rope_q(pair, 1, 1)
+                    add(pair, 1, 4, QH, nc.vector)
+                elif TAIL == 13:
+                    add(pair, 0, 4, RH, nc.vector)
+                    rope_q(pair, 1, 0)
+                    add(pair, 1, QH, RH)
+                    add(pair, 1, 0, 4)
+                    rope_q(pair, 1, 1)
+                    add(pair, 1, 4, QH, nc.vector)
+                elif TAIL == 14:
+                    rope_q(pair, 1, 0)
+                    add(pair, 0, 4, RH, nc.vector)
+                    rope_q(pair, 1, 1)
+                    add(pair, 1, 0, 4, nc.vector)
+                    add(pair, 1, 4, RH, nc.vector)
+                elif TAIL == 15:
+                    pe_add(pair, 0, 4, QH)
+                    add(pair, 0, QH, RH)
+                    rope_q(pair, 1, 0)
+                    rope_q(pair, 1, 1)
+                    add(pair, 1, 0, 4, nc.vector)
+                    add(pair, 1, 4, RH, nc.vector)
+                elif TAIL == 11:
+                    pe_add(pair, 0, 4, QH)
+                    rope_q(pair, 1, 0)
+                    add(pair, 1, 0, 4)
+                    rope_q(pair, 1, 1)
+                    add(pair, 1, 4, QH, nc.vector)
+                elif TAIL == 17:
+                    rope_q(pair, 1, 0)
+                    add(pair, 0, 0, RH, nc.vector)
+                    rope_q(pair, 1, 1)
+                    add(pair, 1, 0, 4, nc.vector)
+                    add(pair, 1, 4, RH, nc.vector)
+                elif TAIL == 18:
+                    rope_q(pair, 1, 0)
+                    add(pair, 0, 0, RH, nc.vector)
+                    add(pair, 1, QH, RH)
+                    rope_q(pair, 1, 1)
+                    add(pair, 1, 0, 4, nc.vector)
                     add(pair, 1, 4, QH, nc.vector)
                 elif TAIL == 6:
                     add(pair, 0, 0, RH)

@@ -393,19 +393,18 @@ def tile_slidingwindowattention_pa_kernel(
             )
 
         def mm_k(pair):
-            psk = psum.tile([P, 2, 2, P], F32, name="psk", tag="bank")
+            psk = psum.tile([P, 2, 1, 2, P], F32, name="psk", tag="bank")
             for cc in range(2):
-                mm(psk[:, cc].rearrange("p h x -> p (h x)"), pair, cc, 2, 0, KF)
+                mm(psk[:, cc].rearrange("p o h x -> p (o h x)"), pair, cc, 2, 0, KF)
             acc[(pair, "k")] = psk
 
         def rope_k(pair):
-            for r in range(2):
-                nc.vector.tensor_tensor(
-                    out=prods[pair][:, :, r, QF:RF].rearrange("p c (h x) -> p c h x", x=P),
-                    in0=acc[(pair, "k")][:],
-                    in1=rot_tab[:, 2 * pair : 2 * pair + 2, r].to_broadcast([P, 2, 2, P]),
-                    op=ALU.mult,
-                )
+            nc.vector.tensor_tensor(
+                out=prods[pair][:, :, :, QF:RF].rearrange("p c r (h x) -> p c r h x", x=P),
+                in0=acc[(pair, "k")][:].to_broadcast([P, 2, 2, 2, P]),
+                in1=rot_tab[:, 2 * pair : 2 * pair + 2].to_broadcast([P, 2, 2, 2, P]),
+                op=ALU.mult,
+            )
 
         def mm_v(pair):
             psv = psum.tile([P, 2, KF], F32, name="psv", tag="bank")
@@ -476,21 +475,19 @@ def tile_slidingwindowattention_pa_kernel(
         warm_pe(W0N)
         x_transpose(0, 0)
         x_transpose(0, 1)
-        w_transpose(0)
+        for a in range(4):
+            w_transpose(a)
         x_transpose(1, 0)
         x_transpose(1, 1)
-        for a in range(1, 4):
-            w_transpose(a)
         for a in range(4):
             w_evac(a)
         x_scale(0, 0)
         x_scale(0, 1)
         table_p(0, 6)
-        x_scale(1, 0)
         x_quant(0)
-        x_scale(1, 1)
         w_quant(0, 0)
-        x_quant(1)
+        x_scale(1, 0)
+        x_scale(1, 1)
         begin(0)
         begin(1)
         for a in range(4, 4 + NW):
@@ -506,6 +503,7 @@ def tile_slidingwindowattention_pa_kernel(
             table_g(6, 12)
         rope_q(0, 0, 0)
         rope_q(0, 1, 0)
+        x_quant(1)
         w_quant(1, 0)
         for a in range(8, 12):
             w_transpose(a)

@@ -40,6 +40,7 @@ NW = 2
 W0N = 4
 WN = 2
 HEAD_BANKS = 16
+LW = (0, 1, 1)
 
 
 def tile_slidingwindowattention_pa_kernel(
@@ -274,12 +275,14 @@ def tile_slidingwindowattention_pa_kernel(
             nc.vector.tensor_copy(out=t[:], in_=xsrc[c].bitcast(FP8))
             xw[c] = t
 
-        def x_transpose(pair, g):
+        def x_transpose(pair, g, mid=0):
             tp = psum.tile([P, 2, 2, P], F32, name="xtp", tag="bank")
             for cc in range(2):
                 words = xw[2 * pair + cc][:].bitcast(F32)
                 for u in range(2):
                     nc.tensor.transpose(tp[:, u, cc, :], words[:, 256 * g + u : 256 * (g + 1) : 2], ident[:])
+                if cc == 0:
+                    warm_pe(mid)
             xtp[(pair, g)] = tp
             after_transposes()
 
@@ -530,8 +533,10 @@ def tile_slidingwindowattention_pa_kernel(
             if pair > 1:
                 begin(pair)
             if prep:
-                x_transpose(nxt, 1)
+                warm_pe(LW[0])
+                x_transpose(nxt, 1, LW[1])
                 x_transpose(nxt, 0)
+                warm_pe(LW[2])
                 if SPAIR <= nxt:
                     x_scale(nxt, 1)
             if 3 <= pair + 2 < NPAIR:

@@ -237,6 +237,22 @@ def tile_slidingwindowattention_pa_kernel(
                 out=tab_blocks[:, a:b, 2, :], in0=tab_blocks[:, a:b, 1, :], scalar1=-1.0, scalar2=None, op0=ALU.mult
             )
 
+        def table_pv(a, b):
+            nc.vector.scalar_tensor_tensor(
+                out=sq[:, a:b, 0, :], in0=sh[:, a:b], scalar=-2.0, in1=sh[:, a:b], op0=ALU.mult, op1=ALU.mult
+            )
+            nc.vector.scalar_tensor_tensor(
+                out=tab_blocks[:, a:b, 1, :], in0=sh[:, a:b], scalar=-2.0, in1=ch[:, a:b], op0=ALU.mult, op1=ALU.mult
+            )
+
+        def table_ps(a, b):
+            nc.scalar.activation(
+                out=tab_blocks[:, a:b, 0:4:3, :], in_=sq[:, a:b].to_broadcast([P, b - a, 2, HALF]), func=ACT.Copy, bias=1.0, scale=1.0
+            )
+            nc.scalar.activation(
+                out=tab_blocks[:, a:b, 2, :], in_=tab_blocks[:, a:b, 1, :], func=ACT.Copy, scale=-1.0
+            )
+
         def table_g(a, b):
             nc.gpsimd.tensor_tensor(out=sq[:, a:b, 0, :], in0=sh[:, a:b], in1=sh[:, a:b], op=ALU.mult)
             nc.gpsimd.tensor_tensor(out=prod[:, a:b, 0, :], in0=sh[:, a:b], in1=ch[:, a:b], op=ALU.mult)
@@ -486,7 +502,8 @@ def tile_slidingwindowattention_pa_kernel(
             w_evac(a)
         x_scale(0, 0)
         x_scale(0, 1)
-        table_p(0, 6)
+        table_pv(0, 6)
+        table_ps(0, 6)
         x_quant(0)
         w_quant(0, 0)
         x_scale(1, 0)
@@ -516,8 +533,8 @@ def tile_slidingwindowattention_pa_kernel(
             w_evac(a)
         x_cast(4)
         x_cast(5)
-        if TAB == 0:
-            table_p(6, 12)
+        table_pv(6, 12)
+        table_ps(6, 12)
         w_quant(2, 0)
         rope_q(0, 0, 1)
         add(0, 0, 0, 4)

@@ -40,6 +40,9 @@ NW = 2
 W0N = 4
 WN = 2
 HEAD_BANKS = 16
+VC3 = 0
+TB1 = 0
+TB2 = 4
 LW = (0, 1, 1)
 
 
@@ -252,6 +255,19 @@ def tile_slidingwindowattention_pa_kernel(
             nc.scalar.activation(
                 out=tab_blocks[:, a:b, 2, :], in_=tab_blocks[:, a:b, 1, :], func=ACT.Copy, scale=-1.0
             )
+
+        absx = const.tile([P, NT, 1, HALF], F32, name="absx")
+        absy = const.tile([P, NT, 1, HALF], F32, name="absy")
+
+        def table_sc(a, b):
+            hp = math.pi / 2.0
+            nc.scalar.activation(out=absx[:, a:b, 0, :], in_=red[:, a:b], func=ACT.Abs)
+            nc.scalar.activation(out=absy[:, a:b, 0, :], in_=red[:, a:b], func=ACT.Abs, bias=-hp)
+            nc.scalar.activation(
+                out=tab_blocks[:, a:b, 0:4:3, :], in_=absx[:, a:b].to_broadcast([P, b - a, 2, HALF]), func=ACT.Sin, bias=hp, scale=-1.0
+            )
+            nc.scalar.activation(out=tab_blocks[:, a:b, 1, :], in_=absy[:, a:b, 0, :], func=ACT.Sin, bias=-hp, scale=1.0)
+            nc.scalar.activation(out=tab_blocks[:, a:b, 2, :], in_=absy[:, a:b, 0, :], func=ACT.Sin, bias=hp, scale=-1.0)
 
         def table_g(a, b):
             nc.gpsimd.tensor_tensor(out=sq[:, a:b, 0, :], in0=sh[:, a:b], in1=sh[:, a:b], op=ALU.mult)
@@ -480,7 +496,8 @@ def tile_slidingwindowattention_pa_kernel(
             x_cast_v(1)
             tv_red(0, 6)
             tv_red(6, 12)
-            table_s(0, 6)
+            if TB1:
+                table_s(0, 6)
         else:
             table_v(0, 2)
             table_s(0, 2)
@@ -489,8 +506,11 @@ def tile_slidingwindowattention_pa_kernel(
             table_s(2, 6)
             table_g(2, 6)
             table_v(6, 12)
-        for c in range(2, 4):
-            x_cast(c)
+        x_cast(2)
+        if VC3:
+            x_cast_v(3)
+        else:
+            x_cast(3)
         warm_pe(W0N)
         x_transpose(0, 0)
         x_transpose(0, 1)
@@ -502,8 +522,11 @@ def tile_slidingwindowattention_pa_kernel(
             w_evac(a)
         x_scale(0, 0)
         x_scale(0, 1)
-        table_pv(0, 6)
-        table_ps(0, 6)
+        if TB1:
+            table_pv(0, 6)
+            table_ps(0, 6)
+        else:
+            table_sc(0, 6)
         x_quant(0)
         w_quant(0, 0)
         x_scale(1, 0)
@@ -518,9 +541,8 @@ def tile_slidingwindowattention_pa_kernel(
             w_transpose(a)
         for a in range(4, 8):
             w_evac(a)
-        table_s(6, 12)
-        if TAB == 1:
-            table_g(6, 12)
+        if TB2 == 0:
+            table_sc(6, 12)
         rope_q(0, 0, 0)
         rope_q(0, 1, 0)
         x_quant(1)
@@ -533,8 +555,8 @@ def tile_slidingwindowattention_pa_kernel(
             w_evac(a)
         x_cast(4)
         x_cast(5)
-        table_pv(6, 12)
-        table_ps(6, 12)
+        if TB2 == 1:
+            table_sc(6, 12)
         w_quant(2, 0)
         rope_q(0, 0, 1)
         add(0, 0, 0, 4)
@@ -571,6 +593,16 @@ def tile_slidingwindowattention_pa_kernel(
                 x_scale(nxt, 0)
             rope_k(pair)
             copy_v(pair)
+            if TB2 == 2 and pair == 1:
+                table_sc(6, 12)
+            if TB2 == 3 and pair == 1:
+                table_sc(6, 9)
+            if TB2 == 3 and pair == 2:
+                table_sc(9, 12)
+            if TB2 == 4 and 1 <= pair <= 3:
+                table_sc(4 + 2 * pair, 6 + 2 * pair)
+            if TB2 == 5 and 0 <= pair <= 2:
+                table_sc(6 + 2 * pair, 8 + 2 * pair)
             if pair == 0:
                 add(pair, 0, QH, RH)
                 add(pair, 1, QH, RH)

@@ -41,6 +41,7 @@ W0N = 4
 WN = 2
 HEAD_BANKS = 16
 VC3 = 0
+WQS = (0, 2)
 TB1 = 0
 TB2 = 4
 LW = (0, 1, 1)
@@ -379,8 +380,24 @@ def tile_slidingwindowattention_pa_kernel(
             r0 = P * (a % 4)
             nc.scalar.copy(out=wg_words[:, :, r0 : r0 + P, :], in_=wtp[a][:].rearrange("p g u r -> p g r u"))
 
+        def w_quant_half(j, half):
+            if half == 0:
+                wq[j] = const.tile([P, NPASS, 512], U32, name="wq%d" % j, align_bytes=64)
+                ws8[j] = const.tile([P, NPASS, 512], U8, name="ws%d" % j, align_bytes=64)
+            cols = slice(256 * half, 256 * (half + 1))
+            for g in range(NPASS):
+                nc.vector.quantize_mx(
+                    out=wq[j][:, g, cols].bitcast(FP8X4),
+                    scales=ws8[j][:, g, cols],
+                    in_=wg[j][:, g, cols, :].rearrange("p f t -> p (f t)"),
+                )
+
         def w_quant(j, g):
             if g == 1:
+                return
+            if j in WQS:
+                w_quant_half(j, 0)
+                w_quant_half(j, 1)
                 return
             wq[j] = const.tile([P, NPASS, 512], U32, name="wq%d" % j, align_bytes=64)
             ws8[j] = const.tile([P, NPASS, 512], U8, name="ws%d" % j, align_bytes=64)

@@ -41,6 +41,7 @@ W0N = 4
 WN = 2
 HEAD_BANKS = 16
 VC3 = 0
+CVE = 1
 WQS = (0, 2)
 TB1 = 0
 TB2 = 4
@@ -595,11 +596,16 @@ def tile_slidingwindowattention_pa_kernel(
                 warm_pe(LW[2])
                 if SPAIR <= nxt:
                     x_scale(nxt, 1)
-            if 3 <= pair + 2 < NPAIR:
+            if 3 <= pair + 2 < NPAIR and not CVE:
                 x_cast(2 * pair + 4)
                 x_cast(2 * pair + 5)
             mm_k(pair)
             mm_v(pair)
+            if CVE:
+                copy_v(pair)
+                if 3 <= pair + 2 < NPAIR:
+                    x_cast(2 * pair + 4)
+                    x_cast(2 * pair + 5)
             if pair > 1 or (pair == 1 and not FILL):
                 mm_q(pair, 0, 0)
             if pair > 0:
@@ -609,7 +615,8 @@ def tile_slidingwindowattention_pa_kernel(
             if prep:
                 x_scale(nxt, 0)
             rope_k(pair)
-            copy_v(pair)
+            if not CVE:
+                copy_v(pair)
             if TB2 == 2 and pair == 1:
                 table_sc(6, 12)
             if TB2 == 3 and pair == 1:

import math
from contextlib import ExitStack

import concourse.mybir as mybir
from concourse.masks import make_identity

F32 = mybir.dt.float32
BF16 = mybir.dt.bfloat16
U8 = mybir.dt.uint8
U32 = mybir.dt.uint32
I32 = mybir.dt.int32
FP8 = mybir.dt.float8_e4m3fn
FP8X4 = mybir.dt.float8_e4m3fn_x4
ALU = mybir.AluOpType
ACT = mybir.ActivationFunctionType

S = 1536
E = 1024
P = 128
NT = S // P
NPAIR = NT // 2
NPASS = E // 512
HALF = 64
THETA = 10000.0
QF = 1024
KF = 256
RF = QF + KF
OF = RF + KF
QH = QF // P
RH = RF // P

FLOPS = 2 * S * E * OF
SPAIR = 2
SPAIR0 = 9
QLATE = 0
FILL = 0
TAIL = 18
TAB = 0
NW = 2
W0N = 4
WN = 2
HEAD_BANKS = 16
VC3 = 0
CVE = 1
WQS = (0, 2)
TB1 = 0
TB2 = 4
LW = (0, 1, 1)


def tile_slidingwindowattention_pa_kernel(
    tc, hidden_states_bytes, hidden_states_scale, q_w, k_w, v_w, out_0, out_1, out_2
):
    nc = tc.nc
    with ExitStack() as ctx:
        const = ctx.enter_context(tc.tile_pool(name="const", bufs=1))
        xwp = ctx.enter_context(tc.tile_pool(name="xwp", bufs=4))
        xgp = ctx.enter_context(tc.tile_pool(name="xgp", bufs=3))
        outp = ctx.enter_context(tc.tile_pool(name="outp", bufs=3))
        prodp = ctx.enter_context(tc.tile_pool(name="prodp", bufs=2))
        psum = ctx.enter_context(tc.psum_pool(name="psum", bufs=8))

        ctx.enter_context(tc.manual_schedule())

        xsc = const.tile([P, NPASS, 1, 4], F32, name="xsc")
        nc.sync.dma_start(
            out=xsc[:, :, 0, :],
            in_=hidden_states_scale.rearrange("a b (g p t) -> p (a b g) t", g=NPASS, p=P, t=4),
        )
        x_rows = hidden_states_bytes.rearrange("b (c p) k -> p (b c) k", p=P)
        q_rows = q_w.rearrange("(a r) k -> r a k", r=P)
        xsrc = {}
        wsrc = {}

        def load_x(lo, hi):
            xb = const.tile([P, hi - lo, E], U8, name="xbytes%d" % lo)
            nc.sync.dma_start(out=xb[:], in_=x_rows[:, lo:hi, :])
            for c in range(lo, hi):
                xsrc[c] = xb[:, c - lo, :]

        def load_w(i):
            wr = const.tile([P, 2, E], BF16, name="wraw%d" % i)
            if i < 4:
                nc.sync.dma_start(out=wr[:], in_=q_rows[:, 2 * i : 2 * i + 2, :])
            elif i == 4:
                nc.sync.dma_start(out=wr[:], in_=k_w.rearrange("(a r) k -> r a k", r=P))
            else:
                nc.sync.dma_start(out=wr[:], in_=v_w.rearrange("(a r) k -> r a k", r=P))
            wsrc[2 * i] = wr[:, 0, :]
            wsrc[2 * i + 1] = wr[:, 1, :]

        load_x(0, 2)
        load_x(2, 4)
        for i in range(4):
            load_w(i)
        load_x(4, 6)
        load_w(4)
        load_w(5)
        load_x(6, 8)
        load_x(8, 12)

        pos = const.tile([P, NT, 1], F32, name="pos")
        nc.gpsimd.iota(
            pos[:], pattern=[[P, NT]], base=0, channel_multiplier=1, allow_small_or_imprecise_dtypes=True
        )
        ident = const.tile([P, P], F32, name="ident")
        make_identity(nc, ident[:])
        warm = const.tile([P, 1], F32, name="warm")
        warm2 = const.tile([P, 1], F32, name="warm2")

        wz = const.tile([P, 512], BF16, name="wz")
        nc.gpsimd.memset(wz[:], 0.0)

        t_banks = [0]

        def after_transposes():
            t_banks[0] += 1
            if t_banks[0] <= HEAD_BANKS and t_banks[0] % 2 == 0:
                warm_pe(WN)

        def warm_pe(n):
            if n == 0:
                return
            t = psum.tile([P, 512], F32, name="pwarm", tag="bank")
            for i in range(n):
                nc.tensor.matmul(out=t[:], lhsT=wz[:, 0:P], rhs=wz[:], start=True, stop=True)

        freq = const.tile([P, 1, HALF], F32, name="freq")
        fab = const.tile([P, 2, 1, 1, 8], F32, name="fab")
        nc.vector.memset(fab[:], 1.0)
        nc.vector.memset(warm[:], 0.0)
        nc.scalar.activation(out=warm2[:], in_=warm[:], func=ACT.Sin)
        for row in (1, 0):
            for j in range(1, 8):
                nc.vector.tensor_scalar(
                    out=fab[:, row, 0, :, j : j + 1],
                    in0=fab[:, 0, 0, :, 0:1],
                    scalar1=THETA ** (-j * (8 if row else 1) / 64.0),
                    scalar2=None,
                    op0=ALU.mult,
                )
        posb = const.tile([P, NT, 8, 1], F32, name="posb")
        tshape = [P, NT, HALF]
        ang = const.tile(tshape, F32, name="ang")
        turns = const.tile(tshape, I32, name="turns")
        red = const.tile(tshape, F32, name="red")
        reda = const.tile(tshape, F32, name="reda")
        sh = const.tile(tshape, F32, name="sh")
        ch = const.tile(tshape, F32, name="ch")
        prod = const.tile([P, NT, 1, HALF], F32, name="prod")
        sq = const.tile([P, NT, 1, HALF], F32, name="sq")
        rot_tab = const.tile([P, NT, 2, 1, P], F32, name="rot_tab")
        tab_blocks = rot_tab[:].rearrange("p c r o (w d) -> p c (r o w) d", d=HALF)

        def table_v(a, b):
            shp = [P, b - a, HALF]
            nc.vector.tensor_tensor(
                out=ang[:, a:b], in0=pos[:, a:b].to_broadcast(shp), in1=freq[:].to_broadcast(shp), op=ALU.mult
            )
            nc.vector.tensor_scalar(
                out=turns[:, a:b], in0=ang[:, a:b], scalar1=1.0 / (2.0 * math.pi), scalar2=0.25, op0=ALU.mult, op1=ALU.add
            )
            nc.vector.scalar_tensor_tensor(
                out=red[:, a:b], in0=turns[:, a:b], scalar=-2.0 * math.pi, in1=ang[:, a:b], op0=ALU.mult, op1=ALU.add
            )
            nc.vector.scalar_tensor_tensor(
                out=reda[:, a:b], in0=red[:, a:b], scalar=-1.0, in1=red[:, a:b], op0=ALU.mult, op1=ALU.max
            )

        def tv_posb(a, b):
            shp = [P, b - a, 8, 1]
            nc.vector.tensor_tensor(
                out=posb[:, a:b],
                in0=pos[:, a:b].rearrange("p c (o i) -> p c o i", i=1).to_broadcast(shp),
                in1=fab[:, 1].rearrange("p a b j -> p a j b").to_broadcast(shp),
                op=ALU.mult,
            )

        def tv_ang(a, b):
            shp = [P, b - a, 8, 8]
            nc.vector.tensor_tensor(
                out=ang[:, a:b].rearrange("p c (i j) -> p c i j", j=8),
                in0=posb[:, a:b].to_broadcast(shp),
                in1=fab[:, 0].to_broadcast(shp),
                op=ALU.mult,
            )

        def tv_turns(a, b):
            nc.vector.tensor_scalar(
                out=turns[:, a:b], in0=ang[:, a:b], scalar1=1.0 / (2.0 * math.pi), scalar2=-0.125, op0=ALU.mult, op1=ALU.add
            )

        def tv_red(a, b):
            nc.vector.scalar_tensor_tensor(
                out=red[:, a:b], in0=turns[:, a:b], scalar=-2.0 * math.pi, in1=ang[:, a:b], op0=ALU.mult, op1=ALU.add
            )

        def tv_abs(a, b):
            nc.vector.scalar_tensor_tensor(
                out=reda[:, a:b], in0=red[:, a:b], scalar=-1.0, in1=red[:, a:b], op0=ALU.mult, op1=ALU.max
            )

        def table_t(a, b):
            nc.scalar.activation(out=turns[:, a:b].bitcast(U32), in_=ang[:, a:b], func=ACT.Copy, bias=0.25, scale=1.0 / (2.0 * math.pi))

        def table_a(a, b):
            shp = [P, b - a, HALF]
            nc.vector.tensor_tensor(
                out=ang[:, a:b], in0=pos[:, a:b].to_broadcast(shp), in1=freq[:].to_broadcast(shp), op=ALU.mult
            )

        def table_r(a, b):
            nc.vector.scalar_tensor_tensor(
                out=red[:, a:b], in0=turns[:, a:b], scalar=-2.0 * math.pi, in1=ang[:, a:b], op0=ALU.mult, op1=ALU.add
            )

        def table_s2(a, b):
            nc.scalar.activation(out=sh[:, a:b], in_=red[:, a:b], func=ACT.Sin, scale=0.5)
            nc.scalar.activation(out=reda[:, a:b], in_=red[:, a:b], func=ACT.Abs)
            nc.scalar.activation(out=ch[:, a:b], in_=reda[:, a:b], func=ACT.Sin, bias=math.pi / 2.0, scale=-0.5)

        def table_s(a, b):
            nc.scalar.activation(out=sh[:, a:b], in_=red[:, a:b], func=ACT.Sin, scale=0.5)
            nc.scalar.activation(out=ch[:, a:b], in_=red[:, a:b], func=ACT.Sin, bias=math.pi / 2.0, scale=-0.5)

        def table_p(a, b):
            n = b - a
            nc.vector.scalar_tensor_tensor(
                out=sq[:, a:b, 0, :], in0=sh[:, a:b], scalar=-2.0, in1=sh[:, a:b], op0=ALU.mult, op1=ALU.mult
            )
            nc.vector.scalar_tensor_tensor(
                out=tab_blocks[:, a:b, 1, :], in0=sh[:, a:b], scalar=-2.0, in1=ch[:, a:b], op0=ALU.mult, op1=ALU.mult
            )
            nc.vector.tensor_scalar(
                out=tab_blocks[:, a:b, 0:4:3, :],
                in0=sq[:, a:b].to_broadcast([P, n, 2, HALF]),
                scalar1=1.0,
                scalar2=None,
                op0=ALU.add,
            )
            nc.vector.tensor_scalar(
                out=tab_blocks[:, a:b, 2, :], in0=tab_blocks[:, a:b, 1, :], scalar1=-1.0, scalar2=None, op0=ALU.mult
            )

        def table_pv(a, b):
            nc.vector.scalar_tensor_tensor(
                out=sq[:, a:b, 0, :], in0=sh[:, a:b], scalar=-2.0, in1=sh[:, a:b], op0=ALU.mult, op1=ALU.mult
            )
            nc.vector.scalar_tensor_tensor(
                out=tab_blocks[:, a:b, 1, :], in0=sh[:, a:b], scalar=-2.0, in1=ch[:, a:b], op0=ALU.mult, op1=ALU.mult
            )

        def table_ps(a, b):
            nc.scalar.activation(
                out=tab_blocks[:, a:b, 0:4:3, :], in_=sq[:, a:b].to_broadcast([P, b - a, 2, HALF]), func=ACT.Copy, bias=1.0, scale=1.0
            )
            nc.scalar.activation(
                out=tab_blocks[:, a:b, 2, :], in_=tab_blocks[:, a:b, 1, :], func=ACT.Copy, scale=-1.0
            )

        absx = const.tile([P, NT, 1, HALF], F32, name="absx")
        absy = const.tile([P, NT, 1, HALF], F32, name="absy")

        def table_sc(a, b):
            hp = math.pi / 2.0
            nc.scalar.activation(out=absx[:, a:b, 0, :], in_=red[:, a:b], func=ACT.Abs)
            nc.scalar.activation(out=absy[:, a:b, 0, :], in_=red[:, a:b], func=ACT.Abs, bias=-hp)
            nc.scalar.activation(
                out=tab_blocks[:, a:b, 0:4:3, :], in_=absx[:, a:b].to_broadcast([P, b - a, 2, HALF]), func=ACT.Sin, bias=hp, scale=-1.0
            )
            nc.scalar.activation(out=tab_blocks[:, a:b, 1, :], in_=absy[:, a:b, 0, :], func=ACT.Sin, bias=-hp, scale=1.0)
            nc.scalar.activation(out=tab_blocks[:, a:b, 2, :], in_=absy[:, a:b, 0, :], func=ACT.Sin, bias=hp, scale=-1.0)

        def table_g(a, b):
            nc.gpsimd.tensor_tensor(out=sq[:, a:b, 0, :], in0=sh[:, a:b], in1=sh[:, a:b], op=ALU.mult)
            nc.gpsimd.tensor_tensor(out=prod[:, a:b, 0, :], in0=sh[:, a:b], in1=ch[:, a:b], op=ALU.mult)
            nc.gpsimd.tensor_scalar(
                out=tab_blocks[:, a:b, 0:4:3, :],
                in0=sq[:, a:b].to_broadcast([P, b - a, 2, HALF]),
                scalar1=-2.0,
                scalar2=1.0,
                op0=ALU.mult,
                op1=ALU.add,
            )
            nc.gpsimd.tensor_scalar(
                out=tab_blocks[:, a:b, 1, :], in0=prod[:, a:b, 0, :], scalar1=-2.0, scalar2=0.0, op0=ALU.mult, op1=ALU.add
            )
            nc.gpsimd.tensor_scalar(
                out=tab_blocks[:, a:b, 2, :], in0=prod[:, a:b, 0, :], scalar1=2.0, scalar2=0.0, op0=ALU.mult, op1=ALU.add
            )

        xw = {}
        xtp = {}
        xg = {}
        xq = {}
        xs8 = {}
        wtp = {}
        wg = {}
        wq = {}
        ws8 = {}

        def x_cast(c):
            t = xwp.tile([P, E], BF16, name="xw", tag="xw")
            nc.scalar.copy(out=t[:], in_=xsrc[c].bitcast(FP8))
            xw[c] = t

        def x_cast_v(c):
            t = xwp.tile([P, E], BF16, name="xw", tag="xw")
            nc.vector.tensor_copy(out=t[:], in_=xsrc[c].bitcast(FP8))
            xw[c] = t

        def x_transpose(pair, g, mid=0):
            tp = psum.tile([P, 2, 2, P], F32, name="xtp", tag="bank")
            for cc in range(2):
                words = xw[2 * pair + cc][:].bitcast(F32)
                for u in range(2):
                    nc.tensor.transpose(tp[:, u, cc, :], words[:, 256 * g + u : 256 * (g + 1) : 2], ident[:])
                if cc == 0:
                    warm_pe(mid)
            xtp[(pair, g)] = tp
            after_transposes()

        def x_transpose_first():
            for g in range(NPASS):
                xtp[(0, g)] = psum.tile([P, 2, 2, P], F32, name="xtp", tag="bank")
            for cc in range(2):
                words = xw[cc][:].bitcast(F32)
                for g in range(NPASS):
                    for u in range(2):
                        nc.tensor.transpose(xtp[(0, g)][:, u, cc, :], words[:, 256 * g + u : 256 * (g + 1) : 2], ident[:])
            after_transposes()
            after_transposes()

        def x_scale_s(pair, g):
            src = xtp[(pair, g)][:].rearrange("p u c n -> p u (c n)").bitcast(BF16).rearrange("p u (n e) -> p u e n", e=2)
            for u in range(2):
                for e in range(2):
                    t = 2 * u + e
                    nc.scalar.activation(
                        out=xg[pair][:, g, :, t], in_=src[:, u, e, :], func=ACT.Copy, scale=xsc[:, g, 0, t : t + 1]
                    )

        def x_scale(pair, g):
            if pair not in xg:
                xg[pair] = xgp.tile([P, NPASS, 2 * P, 4], BF16, name="xg", tag="xg", align_bytes=64)
            if (g == 1 and pair >= SPAIR) or (g == 0 and pair >= SPAIR0):
                x_scale_s(pair, g)
                return
            nc.vector.tensor_tensor(
                out=xg[pair][:, g].rearrange("p n (u e) -> p n u e", e=2),
                in0=xtp[(pair, g)][:].rearrange("p u c n -> p u (c n)").bitcast(BF16).rearrange("p u (n e) -> p n u e", e=2),
                in1=xsc[:, g].rearrange("p o (u e) -> p o u e", e=2).to_broadcast([P, 2 * P, 2, 2]),
                op=ALU.mult,
            )

        def x_quant(pair):
            q = const.tile([P, NPASS * 2 * P], U32, name="xq%d" % pair, align_bytes=64)
            s = const.tile([P, NPASS * 2 * P], U8, name="xs%d" % pair, align_bytes=64)
            nc.vector.quantize_mx(
                out=q[:].bitcast(FP8X4), scales=s[:], in_=xg[pair][:].rearrange("p g n t -> p (g n t)")
            )
            xq[pair] = q
            xs8[pair] = s

        def w_transpose(a):
            words = wsrc[a].bitcast(F32)
            tp = psum.tile([P, NPASS, 2, P], F32, name="wtp", tag="bank")
            for g in range(NPASS):
                for u in range(2):
                    nc.tensor.transpose(tp[:, g, u, :], words[:, 256 * g + u : 256 * (g + 1) : 2], ident[:])
            wtp[a] = tp
            after_transposes()

        def w_evac(a):
            j = a // 4
            if a % 4 == 0:
                wg[j] = const.tile([P, NPASS, 512, 4], BF16, name="wg%d" % j, align_bytes=64)
            wg_words = (
                wg[j][:].rearrange("p g f t -> p (g f t)").bitcast(F32).rearrange("p (g f u) -> p g f u", g=NPASS, u=2)
            )
            r0 = P * (a % 4)
            nc.scalar.copy(out=wg_words[:, :, r0 : r0 + P, :], in_=wtp[a][:].rearrange("p g u r -> p g r u"))

        def w_quant_half(j, half):
            if half == 0:
                wq[j] = const.tile([P, NPASS, 512], U32, name="wq%d" % j, align_bytes=64)
                ws8[j] = const.tile([P, NPASS, 512], U8, name="ws%d" % j, align_bytes=64)
            cols = slice(256 * half, 256 * (half + 1))
            for g in range(NPASS):
                nc.vector.quantize_mx(
                    out=wq[j][:, g, cols].bitcast(FP8X4),
                    scales=ws8[j][:, g, cols],
                    in_=wg[j][:, g, cols, :].rearrange("p f t -> p (f t)"),
                )

        def w_quant(j, g):
            if g == 1:
                return
            if j in WQS:
                w_quant_half(j, 0)
                w_quant_half(j, 1)
                return
            wq[j] = const.tile([P, NPASS, 512], U32, name="wq%d" % j, align_bytes=64)
            ws8[j] = const.tile([P, NPASS, 512], U8, name="ws%d" % j, align_bytes=64)
            nc.vector.quantize_mx(
                out=wq[j][:].rearrange("p g f -> p (g f)").bitcast(FP8X4),
                scales=ws8[j][:].rearrange("p g f -> p (g f)"),
                in_=wg[j][:].rearrange("p g f t -> p (g f t)"),
            )

        def mm(out, pair, cc, j, lo, hi):
            for g in range(NPASS):
                xcols = slice(P * (2 * g + cc), P * (2 * g + cc + 1))
                nc.tensor.matmul_mx(
                    out=out,
                    lhsT=xq[pair][:, xcols].bitcast(FP8X4),
                    lhsT_scale=xs8[pair][:, xcols],
                    rhs=wq[j][:, g, lo:hi].bitcast(FP8X4),
                    rhs_scale=ws8[j][:, g, lo:hi],
                    start=(g == 0),
                    stop=(g == NPASS - 1),
                )

        q_out = out_0.rearrange("b h (c p) d -> c p (b h) d", p=P)
        k_out = out_1.rearrange("b h (c p) d -> c p (b h) d", p=P)
        v_out = out_2.rearrange("b h (c p) d -> c p (b h) d", p=P)
        res = {}
        prods = {}
        acc = {}

        def begin(pair):
            res[pair] = outp.tile([P, 2, OF], F32, name="res", tag="res")
            prods[pair] = prodp.tile([P, 2, 2, RF], F32, name="prods", tag="prods")

        def mm_q(pair, cc, j):
            ps = psum.tile([P, 1, 4, P], F32, name="ps", tag="bank")
            mm(ps[:].rearrange("p o h x -> p (o h x)"), pair, cc, j, 0, 512)
            acc[(pair, cc, j)] = ps

        def rope_q(pair, cc, j):
            nc.vector.tensor_tensor(
                out=prods[pair][:, cc, :, 512 * j : 512 * (j + 1)].rearrange("p r (h x) -> p r h x", x=P),
                in0=acc[(pair, cc, j)][:].to_broadcast([P, 2, 4, P]),
                in1=rot_tab[:, 2 * pair + cc].to_broadcast([P, 2, 4, P]),
                op=ALU.mult,
            )

        def mm_k(pair):
            psk = psum.tile([P, 2, 1, 2, P], F32, name="psk", tag="bank")
            for cc in range(2):
                mm(psk[:, cc].rearrange("p o h x -> p (o h x)"), pair, cc, 2, 0, KF)
            acc[(pair, "k")] = psk

        def rope_k(pair):
            nc.vector.tensor_tensor(
                out=prods[pair][:, :, :, QF:RF].rearrange("p c r (h x) -> p c r h x", x=P),
                in0=acc[(pair, "k")][:].to_broadcast([P, 2, 2, 2, P]),
                in1=rot_tab[:, 2 * pair : 2 * pair + 2].to_broadcast([P, 2, 2, 2, P]),
                op=ALU.mult,
            )

        def mm_v(pair):
            psv = psum.tile([P, 2, KF], F32, name="psv", tag="bank")
            for cc in range(2):
                mm(psv[:, cc, :], pair, cc, 2, KF, 2 * KF)
            acc[(pair, "v")] = psv

        def copy_v(pair):
            nc.scalar.copy(out=res[pair][:, :, RF:OF], in_=acc[(pair, "v")][:])
            for cc in range(2):
                nc.sync.dma_start(
                    out=v_out[2 * pair + cc], in_=res[pair][:, cc, RF:OF].rearrange("p (h d) -> p h d", d=P)
                )

        def pe_add(pair, cc, h0, h1):
            pad = psum.tile([P, P * (h1 - h0)], F32, name="pad", tag="bank")
            u = prods[pair][:, cc, :, P * h0 : P * h1].rearrange("p r (h w d) -> p w h r d", w=2, d=HALF)
            for w in range(2):
                nc.tensor.matmul(
                    out=pad[:].rearrange("p (h r d) -> p h r d", r=2, d=HALF),
                    lhsT=ident[:],
                    rhs=u[:, w],
                    start=(w == 0),
                    stop=(w == 1),
                )
            nc.scalar.copy(out=res[pair][:, cc, P * h0 : P * h1], in_=pad[:])
            nc.sync.dma_start(
                out=q_out[2 * pair + cc][:, h0:h1, :], in_=res[pair][:, cc, P * h0 : P * h1].rearrange("p (h d) -> p h d", d=P)
            )

        def add(pair, cc, h0, h1, eng=None):
            u = prods[pair][:, cc, :, P * h0 : P * h1].rearrange("p r (h w d) -> p r h w d", w=2, d=HALF)
            (eng or nc.gpsimd).tensor_tensor(
                out=res[pair][:, cc, P * h0 : P * h1].rearrange("p (h r d) -> p r h d", r=2, d=HALF),
                in0=u[:, :, :, 0, :],
                in1=u[:, :, :, 1, :],
                op=ALU.add,
            )
            c = 2 * pair + cc
            if h0 < QH:
                hq = min(h1, QH)
                nc.sync.dma_start(
                    out=q_out[c][:, h0:hq, :], in_=res[pair][:, cc, P * h0 : P * hq].rearrange("p (h d) -> p h d", d=P)
                )
            if h1 > QH:
                nc.sync.dma_start(out=k_out[c], in_=res[pair][:, cc, QF:RF].rearrange("p (h d) -> p h d", d=P))

        if TAB == 0:
            nc.scalar.copy(out=wz[:, 0:8], in_=xsc[:].rearrange("p g o t -> p (g o t)"))
            x_cast(0)
            for step in (tv_posb, tv_ang, tv_turns):
                step(0, 6)
                step(6, 12)
            x_cast_v(1)
            tv_red(0, 6)
            tv_red(6, 12)
            if TB1:
                table_s(0, 6)
        else:
            table_v(0, 2)
            table_s(0, 2)
            table_g(0, 2)
            table_v(2, 6)
            table_s(2, 6)
            table_g(2, 6)
            table_v(6, 12)
        x_cast(2)
        if VC3:
            x_cast_v(3)
        else:
            x_cast(3)
        warm_pe(W0N)
        x_transpose(0, 0)
        x_transpose(0, 1)
        for a in range(4):
            w_transpose(a)
        x_transpose(1, 0)
        x_transpose(1, 1)
        for a in range(4):
            w_evac(a)
        x_scale(0, 0)
        x_scale(0, 1)
        if TB1:
            table_pv(0, 6)
            table_ps(0, 6)
        else:
            table_sc(0, 6)
        x_quant(0)
        w_quant(0, 0)
        x_scale(1, 0)
        x_scale(1, 1)
        begin(0)
        begin(1)
        for a in range(4, 4 + NW):
            w_transpose(a)
        mm_q(0, 0, 0)
        mm_q(0, 1, 0)
        for a in range(4 + NW, 8):
            w_transpose(a)
        for a in range(4, 8):
            w_evac(a)
        if TB2 == 0:
            table_sc(6, 12)
        rope_q(0, 0, 0)
        rope_q(0, 1, 0)
        x_quant(1)
        w_quant(1, 0)
        for a in range(8, 12):
            w_transpose(a)
        mm_q(0, 0, 1)
        mm_q(0, 1, 1)
        for a in range(8, 12):
            w_evac(a)
        x_cast(4)
        x_cast(5)
        if TB2 == 1:
            table_sc(6, 12)
        w_quant(2, 0)
        rope_q(0, 0, 1)
        add(0, 0, 0, 4)
        add(0, 0, 4, QH)
        rope_q(0, 1, 1)
        add(0, 1, 0, 4)
        add(0, 1, 4, QH)

        for pair in range(NPAIR):
            last = pair == NPAIR - 1
            nxt = pair + 1
            prep = 2 <= nxt < NPAIR
            if pair > 1:
                begin(pair)
            if prep:
                warm_pe(LW[0])
                x_transpose(nxt, 1, LW[1])
                x_transpose(nxt, 0)
                warm_pe(LW[2])
                if SPAIR <= nxt:
                    x_scale(nxt, 1)
            if 3 <= pair + 2 < NPAIR and not CVE:
                x_cast(2 * pair + 4)
                x_cast(2 * pair + 5)
            mm_k(pair)
            mm_v(pair)
            if CVE:
                copy_v(pair)
                if 3 <= pair + 2 < NPAIR:
                    x_cast(2 * pair + 4)
                    x_cast(2 * pair + 5)
            if pair > 1 or (pair == 1 and not FILL):
                mm_q(pair, 0, 0)
            if pair > 0:
                mm_q(pair, 0, 1)
                mm_q(pair, 1, 0)
                mm_q(pair, 1, 1)
            if prep:
                x_scale(nxt, 0)
            rope_k(pair)
            if not CVE:
                copy_v(pair)
            if TB2 == 2 and pair == 1:
                table_sc(6, 12)
            if TB2 == 3 and pair == 1:
                table_sc(6, 9)
            if TB2 == 3 and pair == 2:
                table_sc(9, 12)
            if TB2 == 4 and 1 <= pair <= 3:
                table_sc(4 + 2 * pair, 6 + 2 * pair)
            if TB2 == 5 and 0 <= pair <= 2:
                table_sc(6 + 2 * pair, 8 + 2 * pair)
            if pair == 0:
                add(pair, 0, QH, RH)
                add(pair, 1, QH, RH)
            if prep and SPAIR > nxt:
                x_scale(nxt, 1)
            if pair > 1 or (pair == 1 and not FILL):
                rope_q(pair, 0, 0)
            if prep and nxt < SPAIR0:
                x_quant(nxt)
            if last and TAIL == 11:
                add(pair, 0, QH, RH)
                add(pair, 1, QH, RH)
            if pair > 0 and (not last or 10 <= TAIL <= 15):
                add(pair, 0, 0, 4)
            if pair > 0:
                rope_q(pair, 0, 1)
                if not last:
                    add(pair, 0, 4, RH)
                    rope_q(pair, 1, 0)
                    if prep and nxt >= SPAIR0:
                        x_quant(nxt)
                    add(pair, 1, 0, 4)
                    rope_q(pair, 1, 1)
                    add(pair, 1, 4, RH)
                elif TAIL == 0:
                    add(pair, 0, 0, RH)
                    rope_q(pair, 1, 0)
                    add(pair, 1, QH, RH)
                    add(pair, 1, 0, 4)
                    rope_q(pair, 1, 1)
                    add(pair, 1, 4, QH)
                elif TAIL == 3:
                    add(pair, 0, 0, RH)
                    rope_q(pair, 1, 0)
                    rope_q(pair, 1, 1)
                    add(pair, 1, 0, RH, nc.vector)
                elif TAIL == 4:
                    add(pair, 0, 0, RH, nc.vector)
                    rope_q(pair, 1, 0)
                    rope_q(pair, 1, 1)
                    add(pair, 1, 0, RH, nc.vector)
                elif TAIL == 5:
                    add(pair, 0, 0, RH, nc.vector)
                    rope_q(pair, 1, 0)
                    add(pair, 1, QH, RH)
                    add(pair, 1, 0, 4)
                    rope_q(pair, 1, 1)
                    add(pair, 1, 4, QH, nc.vector)
                elif TAIL == 10:
                    pe_add(pair, 0, 4, QH)
                    add(pair, 0, QH, RH)
                    rope_q(pair, 1, 0)
                    add(pair, 1, QH, RH)
                    add(pair, 1, 0, 4)
                    rope_q(pair, 1, 1)
                    add(pair, 1, 4, QH, nc.vector)
                elif TAIL == 13:
                    add(pair, 0, 4, RH, nc.vector)
                    rope_q(pair, 1, 0)
                    add(pair, 1, QH, RH)
                    add(pair, 1, 0, 4)
                    rope_q(pair, 1, 1)
                    add(pair, 1, 4, QH, nc.vector)
                elif TAIL == 14:
                    rope_q(pair, 1, 0)
                    add(pair, 0, 4, RH, nc.vector)
                    rope_q(pair, 1, 1)
                    add(pair, 1, 0, 4, nc.vector)
                    add(pair, 1, 4, RH, nc.vector)
                elif TAIL == 15:
                    pe_add(pair, 0, 4, QH)
                    add(pair, 0, QH, RH)
                    rope_q(pair, 1, 0)
                    rope_q(pair, 1, 1)
                    add(pair, 1, 0, 4, nc.vector)
                    add(pair, 1, 4, RH, nc.vector)
                elif TAIL == 11:
                    pe_add(pair, 0, 4, QH)
                    rope_q(pair, 1, 0)
                    add(pair, 1, 0, 4)
                    rope_q(pair, 1, 1)
                    add(pair, 1, 4, QH, nc.vector)
                elif TAIL == 17:
                    rope_q(pair, 1, 0)
                    add(pair, 0, 0, RH, nc.vector)
                    rope_q(pair, 1, 1)
                    add(pair, 1, 0, 4, nc.vector)
                    add(pair, 1, 4, RH, nc.vector)
                elif TAIL == 18:
                    rope_q(pair, 1, 0)
                    add(pair, 0, 0, RH, nc.vector)
                    add(pair, 1, QH, RH)
                    rope_q(pair, 1, 1)
                    add(pair, 1, 0, 4, nc.vector)
                    add(pair, 1, 4, QH, nc.vector)
                elif TAIL == 6:
                    add(pair, 0, 0, RH)
                    rope_q(pair, 1, 0)
                    rope_q(pair, 1, 1)
                    add(pair, 1, 4, RH, nc.vector)
                    add(pair, 1, 0, 4, nc.vector)
